import numpy as np
import ml_dtypes


BF16 = ml_dtypes.bfloat16


def bf(x):
    return np.asarray(x, np.float32).astype(BF16)


def f64(x):
    return np.asarray(x).astype(np.float64)


E2M1 = np.array([0.0, 0.5, 1.0, 1.5, 2.0, 3.0, 4.0, 6.0, -0.0, -0.5, -1.0, -1.5, -2.0, -3.0, -4.0, -6.0])


def pack_weight(w, fmt):
    k, n = w.shape
    w = f64(bf(w)).reshape(k // 32, 32, n)
    amax = np.abs(w).max(1)
    if fmt == "e4m3":
        byte = np.frexp(amax)[1] - 1 + 127 - 7
    else:
        mant, ex = np.frexp(amax / 6.0)
        byte = np.where(mant > 0.5, ex, ex - 1) + 127
    byte = np.clip(np.where(amax > 0, byte, 1), 1, 254)
    scaled = (w * np.exp2(127.0 - byte)[:, None, :]).reshape(k, n).astype(np.float32)
    by_word = np.ascontiguousarray(scaled.reshape(k // 512, 128, 4, n).transpose(0, 1, 3, 2))
    if fmt == "e4m3":
        words = by_word.astype(ml_dtypes.float8_e4m3fn).view(np.uint8)
    else:
        c = by_word.astype(ml_dtypes.float4_e2m1fn).view(np.uint8) & 0xF
        words = c[..., 0::2] | (c[..., 1::2] << 4)
    return np.ascontiguousarray(words), np.ascontiguousarray(byte.astype(np.uint8).reshape(k // 512, 16, n))


def unpack_weight(words, scales, fmt):
    g, p, n, _ = words.shape
    if fmt == "e4m3":
        vals = np.ascontiguousarray(words).view(ml_dtypes.float8_e4m3fn).astype(np.float64)
    else:
        nib = np.empty((g, p, n, 4), np.uint8)
        nib[..., 0::2] = words & 0xF
        nib[..., 1::2] = words >> 4
        vals = E2M1[nib]
    vals = vals * np.repeat(np.exp2(scales.astype(np.float64) - 127.0), 8, axis=1)[..., None]
    return vals.transpose(0, 1, 3, 2).reshape(g * 512, n)

def pack4(w):
    words, scales = pack_weight(w, "e2m1")
    return words.reshape(words.shape[0], 128, -1), scales


def unpack4(words, scales):
    return unpack_weight(words.reshape(words.shape[0], 128, -1, 2), scales, "e2m1")


def kspread(k):
    return np.exp2(np.repeat(np.random.randint(-6, 7, k // 32), 32).astype(np.float64))


B, T, C, N_HEAD, N_KV, HD, WINDOW = 1, 2048, 4096, 8, 2, 256, 512
QPK = N_HEAD // N_KV
TOT = QPK + 2
QKV_OUT = N_KV * TOT * HD


def apply_rope(xh, fc):
    b, t, h, d = xh.shape
    xs = xh.reshape(b, t, h, d // 2, 2)
    f = fc.reshape(1, t, 1, d // 2, 2)
    re = xs[..., 0] * f[..., 0] - xs[..., 1] * f[..., 1]
    im = xs[..., 1] * f[..., 0] + xs[..., 0] * f[..., 1]
    return np.stack([re, im], axis=-1).reshape(b, t, h, d)


def setup_inputs():
    s = kspread(C)
    inv_freq = 1.0 / (10000.0 ** (np.arange(0, HD, 2) / HD))
    ang = np.outer(np.arange(T), inv_freq)
    x = np.random.standard_normal((B, T, C)) * s
    x_words, x_scales = pack4(x.reshape(B * T, C).T)
    freqs_cis = bf(np.stack([np.cos(ang), np.sin(ang)], axis=-1))
    words, scales = pack4(np.random.standard_normal((C, QKV_OUT)) * 1.5 / np.sqrt(C) / s[:, None])
    return {"x_words": x_words,
            "x_scales": x_scales,
            "freqs_cis": freqs_cis,
            "W_attn_words": words,
            "W_attn_scales": scales}


def reference(x_words, x_scales, freqs_cis, W_attn_words, W_attn_scales):
    x = unpack4(x_words, x_scales).T.reshape(B, T, C)
    qkv = x @ unpack4(W_attn_words, W_attn_scales)
    qkv = qkv.reshape(B, T, N_KV, TOT, HD).transpose(0, 2, 3, 1, 4)
    q = qkv[:, :, :QPK].reshape(B, -1, N_HEAD, HD)
    k = qkv[:, :, QPK:QPK + 1].reshape(B, -1, N_KV, HD)
    v = qkv[:, :, QPK + 1:].reshape(B, -1, N_KV, HD)
    fc = f64(freqs_cis)
    return apply_rope(q, fc), apply_rope(k, fc), v

@@ -1,0 +1,265 @@
+from contextlib import ExitStack
+
+import concourse.mybir as mybir
+
+F32 = mybir.dt.float32
+BF16 = mybir.dt.bfloat16
+I32 = mybir.dt.int32
+U8 = mybir.dt.uint8
+FP4X4 = mybir.dt.float4_e2m1fn_x4
+MULT = mybir.AluOpType.mult
+ADD = mybir.AluOpType.add
+COPY = mybir.ActivationFunctionType.Copy
+
+P = 128
+TOKENS = 2048
+K = 4096
+COLS = 3072
+HD = 256
+PASSES = K // 512
+TILES = TOKENS // P
+BLOCK = 512
+FLOPS = 2 * TOKENS * K * COLS
+
+BLOCKS = [("kv", 1024, 0), ("q", 0, 0), ("q", 512, 2), ("q", 1536, 4), ("q", 2048, 6), ("kv", 2560, 1)]
+
+
+def tile_causalselfattentiongqa_pa_kernel(
+    tc, x_words, x_scales, freqs_cis, W_words, W_scales, out_q, out_k, out_v
+):
+    nc = tc.nc
+
+    q_rows = out_q.rearrange("b n h c -> (b n h) c").rearrange("(s t p) c -> s t p c", s=8, p=P)
+    k_rows = out_k.rearrange("b n h c -> (b n h) c").rearrange("(s t p) c -> s t p c", s=2, p=P)
+    v_rows = out_v.rearrange("b n h c -> (b n h) c").rearrange("(s t p) c -> s t p c", s=2, p=P)
+    freq_rows = freqs_cis.rearrange("n i e -> n (i e)")
+    freq_q = freq_rows.rearrange("(j r) c -> r j c", r=16)
+    freq_k = freq_rows.rearrange("(j r) c -> r j c", r=64)
+
+    with ExitStack() as ctx:
+        keep = ctx.enter_context(tc.tile_pool(name="keep", bufs=1))
+        tab = ctx.enter_context(tc.tile_pool(name="tab", bufs=2))
+        work = ctx.enter_context(tc.tile_pool(name="work", bufs=3))
+        outs = ctx.enter_context(tc.tile_pool(name="outs", bufs=6))
+        psum = ctx.enter_context(tc.psum_pool(name="psum", bufs=8))
+        ctx.enter_context(tc.manual_schedule())
+
+        def load_codes(codes, words, g0, g1, c0, cols):
+            nc.sync.dma_start(
+                out=codes[:, g0:g1, :].bitcast(I32),
+                in_=words[g0:g1, :, 2 * c0 : 2 * (c0 + cols)].rearrange("g p n -> p g n").bitcast(I32),
+            )
+
+        def load_scales(planes, scales, g0, g1, c0, cols):
+            for q in range(4):
+                nc.sync.dma_start(
+                    out=planes[32 * q : 32 * q + 4, g0:g1, :].bitcast(I32),
+                    in_=scales[g0:g1, 4 * q : 4 * q + 4, c0 : c0 + cols].rearrange("g r n -> r g n").bitcast(I32),
+                )
+
+        def zero(engine, planes, g0, g1):
+            engine.memset(planes[:, g0:g1, :].bitcast(I32), 0)
+
+        half = TOKENS // 2
+        xa = keep.tile([P, PASSES, 2 * half], U8, name="xa", align_bytes=64)
+        xb = keep.tile([P, PASSES, half], U8, name="xb", align_bytes=64)
+        xc = keep.tile([P, PASSES, half], U8, name="xc", align_bytes=64)
+        xsa = keep.tile([P, PASSES, half], U8, name="xsa", align_bytes=64)
+        xsb = keep.tile([P, PASSES, half], U8, name="xsb", align_bytes=64)
+        wc = [keep.tile([P, PASSES, 2 * BLOCK], U8, name=f"wc{b}", align_bytes=64) for b in range(6)]
+        ws = [keep.tile([P, PASSES, BLOCK], U8, name=f"ws{b}", align_bytes=64) for b in range(6)]
+        kf = [keep.tile([P, TILES, HD], BF16, name=f"kf{b}") for b in range(2)]
+
+        def stationary(t, g):
+            if t < 8:
+                return xa[:, g, 256 * t : 256 * (t + 1)], xsa[:, g, P * t : P * (t + 1)]
+            u = t - 8
+            codes = xb if u < 4 else xc
+            return codes[:, g, 256 * (u % 4) : 256 * (u % 4 + 1)], xsb[:, g, P * u : P * (u + 1)]
+
+        def multiply(acc, b, t, g, c0=0, cols=BLOCK):
+            codes, planes = stationary(t, g)
+            nc.tensor.matmul_mx(
+                out=acc,
+                lhsT=codes.bitcast(FP4X4),
+                lhsT_scale=planes,
+                rhs=wc[b][:, g, 2 * c0 : 2 * (c0 + cols)].bitcast(FP4X4),
+                rhs_scale=ws[b][:, g, c0 : c0 + cols],
+                start=(g == 0),
+                stop=(g == PASSES - 1),
+            )
+
+        dummy = keep.tile([P, BLOCK], BF16, name="dummy")
+        nc.gpsimd.memset(dummy[:], 0.0)
+        zero(nc.vector, ws[0], 0, 2)
+        zero(nc.vector, xsa, 0, 2)
+        zero(nc.vector, ws[0], 2, PASSES)
+        zero(nc.vector, xsa, 2, PASSES)
+        zero(nc.gpsimd, xsb, 0, PASSES)
+        for b in range(1, 6):
+            zero(nc.gpsimd, ws[b], 0, PASSES)
+
+        def load_a(g0, g1):
+            load_codes(wc[0], W_words, g0, g1, BLOCKS[0][1], BLOCK)
+            load_codes(xa, x_words, g0, g1, 0, half)
+
+        load_a(0, 1)
+        load_scales(ws[0], W_scales, 0, 2, BLOCKS[0][1], BLOCK)
+        load_scales(xsa, x_scales, 0, 2, 0, half)
+        load_a(1, 2)
+        load_scales(ws[0], W_scales, 2, PASSES, BLOCKS[0][1], BLOCK)
+        load_scales(xsa, x_scales, 2, PASSES, 0, half)
+        load_a(2, 4)
+        load_a(4, 6)
+        load_a(6, 8)
+
+        warm = psum.tile([P, BLOCK], F32, name="acc")
+        for i in range(8):
+            nc.tensor.matmul(out=warm[:], lhsT=dummy[:, 0:P], rhs=dummy[:], start=True, stop=True)
+
+        q_tables = {}
+
+        def load_tables(b):
+            kind, c0, first = BLOCKS[b]
+            if kind == "q":
+                f = tab.tile([P, 2, TILES, HD], BF16, name="f")
+                q_tables[b] = f
+                for r in range(16):
+                    nc.sync.dma_start(
+                        out=f[8 * r : 8 * r + 8, :, :, :].rearrange("p s t c -> p (s t) c"),
+                        in_=freq_q[r : r + 1, 16 * first : 16 * first + 32, :].to_broadcast([8, 32, HD]),
+                    )
+            else:
+                for h in range(2):
+                    nc.sync.dma_start(
+                        out=kf[first][h:P:2, :, :],
+                        in_=freq_k[:, 16 * first : 16 * first + 16, :],
+                    )
+
+        def load_weights(b):
+            load_scales(ws[b], W_scales, 0, PASSES, BLOCKS[b][1], BLOCK)
+            load_codes(wc[b], W_words, 0, PASSES, BLOCKS[b][1], BLOCK)
+
+        load_tables(0)
+        load_scales(xsb, x_scales, 0, PASSES, half, half)
+        load_codes(xb, x_words, 0, PASSES, half, half // 2)
+        load_codes(xc, x_words, 0, PASSES, half + half // 2, half // 2)
+
+        def table(b, t):
+            kind, c0, first = BLOCKS[b]
+            if kind == "q":
+                return q_tables[b][:, :, t, :].rearrange("p s (i e) -> p s i e", e=2)
+            return kf[first][:, t : t + 1, :].rearrange("p s (i e) -> p s i e", e=2)
+
+        groups = [(b, t) for b in range(6) for t in range(TILES)]
+        signed = {}
+
+        def sign_table(n):
+            if n >= len(groups):
+                return
+            b, t = groups[n]
+            f = table(b, t)
+            slots = f.shape[1]
+            d = work.tile([P, 2, P, 2], BF16, name="d", bufs=6)
+            nc.scalar.activation(out=d[:, 0:slots, :, 0], in_=f[:, :, :, 1], func=COPY, scale=-1.0)
+            nc.scalar.copy(out=d[:, 0:slots, :, 1], in_=f[:, :, :, 1])
+            signed[n] = d
+
+        pending = []
+
+        def flush():
+            while pending:
+                t1, t2, res, stores = pending.pop()
+                nc.vector.tensor_tensor(out=res, in0=t1, in1=t2, op=ADD)
+                for engine, dst, src in stores:
+                    engine.dma_start(out=dst, in_=src)
+
+        def rotate(n, acc, res, stores, between=None):
+            b, t = groups[n]
+            f = table(b, t)
+            slots = f.shape[1]
+            shape = [P, slots, P, 2]
+            a = acc.rearrange("p (s i e) -> p s i e", s=slots, e=2)
+            t1 = work.tile([P, 2, P, 2], F32, name="t1")
+            t2 = work.tile([P, 2, P, 2], F32, name="t2")
+            nc.vector.tensor_tensor(
+                out=t1[:, 0:slots], in0=a, in1=f[:, :, :, 0:1].to_broadcast(shape), op=MULT
+            )
+            nc.vector.tensor_tensor(out=t2[:, 0:slots], in0=a[:, :, :, ::-1], in1=signed[n][:, 0:slots], op=MULT)
+            if between is not None:
+                between()
+            flush()
+            flat = "p s i e -> p (s i e)"
+            pending.append((t1[:, 0:slots].rearrange(flat), t2[:, 0:slots].rearrange(flat), res, stores))
+
+        pair = {}
+
+        def drain(n, acc):
+            b, t = groups[n]
+            kind, c0, first = BLOCKS[b]
+            if kind == "q":
+                o = outs.tile([P, 2, HD], F32, name="o")
+                dst = q_rows[first : first + 2, t].rearrange("s p c -> p s c")
+                rotate(n, acc, o[:].rearrange("p s c -> p (s c)"), [(nc.gpsimd, dst, o[:])])
+                return
+            if t % 2 == 0:
+                pair["k"] = outs.tile([P, 2, HD], F32, name="ko", bufs=3)
+                pair["v"] = outs.tile([P, 2, HD], F32, name="vo", bufs=3)
+            ko, vo = pair["k"], pair["v"]
+            u = t % 2
+            lone = b == 5 and t == TILES - 2
+            if lone:
+                k_store = [(nc.sync, k_rows[first, t], ko[:, 0, :])]
+            elif u == 1:
+                k_store = [(nc.gpsimd, k_rows[first, t - 1 : t + 1].rearrange("t p c -> p t c"), ko[:])]
+            else:
+                k_store = []
+
+            def copy_v():
+                nc.vector.tensor_copy(out=vo[:, u, :], in_=acc[:, HD : 2 * HD])
+                if lone:
+                    nc.sync.dma_start(out=v_rows[first, t], in_=vo[:, 0, :])
+                elif u == 1:
+                    nc.gpsimd.dma_start(out=v_rows[first, t - 1 : t + 1].rearrange("t p c -> p t c"), in_=vo[:])
+
+            rotate(n, acc[:, 0:HD], ko[:, u, :], k_store, copy_v)
+
+        sign_table(0)
+        sign_table(1)
+        accs = []
+        for t in range(8):
+            acc = psum.tile([P, BLOCK], F32, name="acc")
+            accs.append(acc)
+        for g in range(PASSES):
+            for t in range(8):
+                multiply(accs[t][:], 0, t, g)
+        load_weights(1)
+        load_tables(1)
+        for n in range(8):
+            sign_table(n + 2)
+            drain(n, accs[n][:])
+
+        for n in range(8, len(groups) - 1):
+            b, t = groups[n]
+            if t == 0 and b < 5:
+                load_weights(b + 1)
+                load_tables(b + 1)
+            sign_table(n + 2)
+            acc = psum.tile([P, BLOCK], F32, name="acc")
+            for g in range(PASSES):
+                multiply(acc[:], b, t, g)
+            drain(n, acc[:])
+
+        n = len(groups) - 1
+        b, t = groups[n]
+        ko, vo = pair["k"], pair["v"]
+        acc_k = psum.tile([P, BLOCK], F32, name="acc")
+        acc_v = psum.tile([P, BLOCK], F32, name="acc")
+        for g in range(PASSES):
+            multiply(acc_k[:, 0:HD], b, t, g, 0, HD)
+        for g in range(PASSES):
+            multiply(acc_v[:, 0:HD], b, t, g, HD, HD)
+        rotate(n, acc_k[:, 0:HD], ko[:, 1, :], [(nc.sync, k_rows[1, t], ko[:, 1, :])])
+        flush()
+        nc.scalar.copy(out=vo[:, 1, :], in_=acc_v[:, 0:HD])
+        nc.scalar.dma_start(out=v_rows[1, t], in_=vo[:, 1, :])

@@ -124,10 +124,10 @@ def tile_causalselfattentiongqa_pa_kernel(
             if kind == "q":
                 f = tab.tile([P, 2, TILES, HD], BF16, name="f")
                 q_tables[b] = f
-                for r in range(16):
+                for h in range(8):
                     nc.sync.dma_start(
-                        out=f[8 * r : 8 * r + 8, :, :, :].rearrange("p s t c -> p (s t) c"),
-                        in_=freq_q[r : r + 1, 16 * first : 16 * first + 32, :].to_broadcast([8, 32, HD]),
+                        out=f[h:P:8, :, :, :].rearrange("p s t c -> p (s t) c"),
+                        in_=freq_q[:, 16 * first : 16 * first + 32, :],
                     )
             else:
                 for h in range(2):

@@ -51,10 +51,10 @@ def tile_causalselfattentiongqa_pa_kernel(
             )
 
         def load_scales(planes, scales, g0, g1, c0, cols):
-            for q in range(4):
+            for r in range(4):
                 nc.sync.dma_start(
-                    out=planes[32 * q : 32 * q + 4, g0:g1, :].bitcast(I32),
-                    in_=scales[g0:g1, 4 * q : 4 * q + 4, c0 : c0 + cols].rearrange("g r n -> r g n").bitcast(I32),
+                    out=planes[r:P:32, g0:g1, :].bitcast(I32),
+                    in_=scales[g0:g1, r:16:4, c0 : c0 + cols].rearrange("g q n -> q g n").bitcast(I32),
                 )
 
         def zero(engine, planes, g0, g1):
@@ -198,9 +198,11 @@ def tile_causalselfattentiongqa_pa_kernel(
             b, t = groups[n]
             kind, c0, first = BLOCKS[b]
             if kind == "q":
-                o = outs.tile([P, 2, HD], F32, name="o")
+                o = outs.tile([P, 2, HD], F32, name="o", bufs=4)
                 dst = q_rows[first : first + 2, t].rearrange("s p c -> p s c")
-                rotate(n, acc, o[:].rearrange("p s c -> p (s c)"), [(nc.gpsimd, dst, o[:])])
+                u = work.tile([P, BLOCK], F32, name="u", bufs=4)
+                nc.scalar.copy(out=u[:], in_=acc)
+                rotate(n, u[:], o[:].rearrange("p s c -> p (s c)"), [(nc.gpsimd, dst, o[:])])
                 return
             if t % 2 == 0:
                 pair["k"] = outs.tile([P, 2, HD], F32, name="ko", bufs=3)
@@ -215,14 +217,16 @@ def tile_causalselfattentiongqa_pa_kernel(
             else:
                 k_store = []
 
-            def copy_v():
-                nc.vector.tensor_copy(out=vo[:, u, :], in_=acc[:, HD : 2 * HD])
+            def store_v():
                 if lone:
                     nc.sync.dma_start(out=v_rows[first, t], in_=vo[:, 0, :])
                 elif u == 1:
                     nc.gpsimd.dma_start(out=v_rows[first, t - 1 : t + 1].rearrange("t p c -> p t c"), in_=vo[:])
 
-            rotate(n, acc[:, 0:HD], ko[:, u, :], k_store, copy_v)
+            ku = work.tile([P, BLOCK], F32, name="u", bufs=4)
+            nc.scalar.copy(out=ku[:, 0:HD], in_=acc[:, 0:HD])
+            nc.scalar.copy(out=vo[:, u, :], in_=acc[:, HD : 2 * HD])
+            rotate(n, ku[:, 0:HD], ko[:, u, :], k_store, store_v)
 
         sign_table(0)
         sign_table(1)

from contextlib import ExitStack

import concourse.mybir as mybir

F32 = mybir.dt.float32
BF16 = mybir.dt.bfloat16
I32 = mybir.dt.int32
U8 = mybir.dt.uint8
FP4X4 = mybir.dt.float4_e2m1fn_x4
MULT = mybir.AluOpType.mult
ADD = mybir.AluOpType.add
COPY = mybir.ActivationFunctionType.Copy

P = 128
TOKENS = 2048
K = 4096
COLS = 3072
HD = 256
PASSES = K // 512
TILES = TOKENS // P
BLOCK = 512
FLOPS = 2 * TOKENS * K * COLS

BLOCKS = [("kv", 1024, 0), ("q", 0, 0), ("q", 512, 2), ("q", 1536, 4), ("q", 2048, 6), ("kv", 2560, 1)]


def tile_causalselfattentiongqa_pa_kernel(
    tc, x_words, x_scales, freqs_cis, W_words, W_scales, out_q, out_k, out_v
):
    nc = tc.nc

    q_rows = out_q.rearrange("b n h c -> (b n h) c").rearrange("(s t p) c -> s t p c", s=8, p=P)
    k_rows = out_k.rearrange("b n h c -> (b n h) c").rearrange("(s t p) c -> s t p c", s=2, p=P)
    v_rows = out_v.rearrange("b n h c -> (b n h) c").rearrange("(s t p) c -> s t p c", s=2, p=P)
    freq_rows = freqs_cis.rearrange("n i e -> n (i e)")
    freq_q = freq_rows.rearrange("(j r) c -> r j c", r=16)
    freq_k = freq_rows.rearrange("(j r) c -> r j c", r=64)

    with ExitStack() as ctx:
        keep = ctx.enter_context(tc.tile_pool(name="keep", bufs=1))
        tab = ctx.enter_context(tc.tile_pool(name="tab", bufs=2))
        work = ctx.enter_context(tc.tile_pool(name="work", bufs=3))
        outs = ctx.enter_context(tc.tile_pool(name="outs", bufs=6))
        psum = ctx.enter_context(tc.psum_pool(name="psum", bufs=8))
        ctx.enter_context(tc.manual_schedule())

        def load_codes(codes, words, g0, g1, c0, cols):
            nc.sync.dma_start(
                out=codes[:, g0:g1, :].bitcast(I32),
                in_=words[g0:g1, :, 2 * c0 : 2 * (c0 + cols)].rearrange("g p n -> p g n").bitcast(I32),
            )

        def load_scales(planes, scales, g0, g1, c0, cols):
            for r in range(4):
                nc.sync.dma_start(
                    out=planes[r:P:32, g0:g1, :].bitcast(I32),
                    in_=scales[g0:g1, r:16:4, c0 : c0 + cols].rearrange("g q n -> q g n").bitcast(I32),
                )

        def zero(engine, planes, g0, g1):
            engine.memset(planes[:, g0:g1, :].bitcast(I32), 0)

        half = TOKENS // 2
        xa = keep.tile([P, PASSES, 2 * half], U8, name="xa", align_bytes=64)
        xb = keep.tile([P, PASSES, half], U8, name="xb", align_bytes=64)
        xc = keep.tile([P, PASSES, half], U8, name="xc", align_bytes=64)
        xsa = keep.tile([P, PASSES, half], U8, name="xsa", align_bytes=64)
        xsb = keep.tile([P, PASSES, half], U8, name="xsb", align_bytes=64)
        wc = [keep.tile([P, PASSES, 2 * BLOCK], U8, name=f"wc{b}", align_bytes=64) for b in range(6)]
        ws = [keep.tile([P, PASSES, BLOCK], U8, name=f"ws{b}", align_bytes=64) for b in range(6)]
        kf = [keep.tile([P, TILES, HD], BF16, name=f"kf{b}") for b in range(2)]

        def stationary(t, g):
            if t < 8:
                return xa[:, g, 256 * t : 256 * (t + 1)], xsa[:, g, P * t : P * (t + 1)]
            u = t - 8
            codes = xb if u < 4 else xc
            return codes[:, g, 256 * (u % 4) : 256 * (u % 4 + 1)], xsb[:, g, P * u : P * (u + 1)]

        def multiply(acc, b, t, g, c0=0, cols=BLOCK):
            codes, planes = stationary(t, g)
            nc.tensor.matmul_mx(
                out=acc,
                lhsT=codes.bitcast(FP4X4),
                lhsT_scale=planes,
                rhs=wc[b][:, g, 2 * c0 : 2 * (c0 + cols)].bitcast(FP4X4),
                rhs_scale=ws[b][:, g, c0 : c0 + cols],
                start=(g == 0),
                stop=(g == PASSES - 1),
            )

        dummy = keep.tile([P, BLOCK], BF16, name="dummy")
        nc.gpsimd.memset(dummy[:], 0.0)
        zero(nc.vector, ws[0], 0, 2)
        zero(nc.vector, xsa, 0, 2)
        zero(nc.vector, ws[0], 2, PASSES)
        zero(nc.vector, xsa, 2, PASSES)
        zero(nc.gpsimd, xsb, 0, PASSES)
        for b in range(1, 6):
            zero(nc.gpsimd, ws[b], 0, PASSES)

        def load_a(g0, g1):
            load_codes(wc[0], W_words, g0, g1, BLOCKS[0][1], BLOCK)
            load_codes(xa, x_words, g0, g1, 0, half)

        load_a(0, 1)
        load_scales(ws[0], W_scales, 0, 2, BLOCKS[0][1], BLOCK)
        load_scales(xsa, x_scales, 0, 2, 0, half)
        load_a(1, 2)
        load_scales(ws[0], W_scales, 2, PASSES, BLOCKS[0][1], BLOCK)
        load_scales(xsa, x_scales, 2, PASSES, 0, half)
        load_a(2, 4)
        load_a(4, 6)
        load_a(6, 8)

        warm = psum.tile([P, BLOCK], F32, name="acc")
        for i in range(8):
            nc.tensor.matmul(out=warm[:], lhsT=dummy[:, 0:P], rhs=dummy[:], start=True, stop=True)

        q_tables = {}

        def load_tables(b):
            kind, c0, first = BLOCKS[b]
            if kind == "q":
                f = tab.tile([P, 2, TILES, HD], BF16, name="f")
                q_tables[b] = f
                for h in range(8):
                    nc.sync.dma_start(
                        out=f[h:P:8, :, :, :].rearrange("p s t c -> p (s t) c"),
                        in_=freq_q[:, 16 * first : 16 * first + 32, :],
                    )
            else:
                for h in range(2):
                    nc.sync.dma_start(
                        out=kf[first][h:P:2, :, :],
                        in_=freq_k[:, 16 * first : 16 * first + 16, :],
                    )

        def load_weights(b):
            load_scales(ws[b], W_scales, 0, PASSES, BLOCKS[b][1], BLOCK)
            load_codes(wc[b], W_words, 0, PASSES, BLOCKS[b][1], BLOCK)

        load_tables(0)
        load_scales(xsb, x_scales, 0, PASSES, half, half)
        load_codes(xb, x_words, 0, PASSES, half, half // 2)
        load_codes(xc, x_words, 0, PASSES, half + half // 2, half // 2)

        def table(b, t):
            kind, c0, first = BLOCKS[b]
            if kind == "q":
                return q_tables[b][:, :, t, :].rearrange("p s (i e) -> p s i e", e=2)
            return kf[first][:, t : t + 1, :].rearrange("p s (i e) -> p s i e", e=2)

        groups = [(b, t) for b in range(6) for t in range(TILES)]
        signed = {}

        def sign_table(n):
            if n >= len(groups):
                return
            b, t = groups[n]
            f = table(b, t)
            slots = f.shape[1]
            d = work.tile([P, 2, P, 2], BF16, name="d", bufs=6)
            nc.scalar.activation(out=d[:, 0:slots, :, 0], in_=f[:, :, :, 1], func=COPY, scale=-1.0)
            nc.scalar.copy(out=d[:, 0:slots, :, 1], in_=f[:, :, :, 1])
            signed[n] = d

        pending = []

        def flush():
            while pending:
                t1, t2, res, stores = pending.pop()
                nc.vector.tensor_tensor(out=res, in0=t1, in1=t2, op=ADD)
                for engine, dst, src in stores:
                    engine.dma_start(out=dst, in_=src)

        def rotate(n, acc, res, stores, between=None):
            b, t = groups[n]
            f = table(b, t)
            slots = f.shape[1]
            shape = [P, slots, P, 2]
            a = acc.rearrange("p (s i e) -> p s i e", s=slots, e=2)
            t1 = work.tile([P, 2, P, 2], F32, name="t1")
            t2 = work.tile([P, 2, P, 2], F32, name="t2")
            nc.vector.tensor_tensor(
                out=t1[:, 0:slots], in0=a, in1=f[:, :, :, 0:1].to_broadcast(shape), op=MULT
            )
            nc.vector.tensor_tensor(out=t2[:, 0:slots], in0=a[:, :, :, ::-1], in1=signed[n][:, 0:slots], op=MULT)
            if between is not None:
                between()
            flush()
            flat = "p s i e -> p (s i e)"
            pending.append((t1[:, 0:slots].rearrange(flat), t2[:, 0:slots].rearrange(flat), res, stores))

        pair = {}

        def drain(n, acc):
            b, t = groups[n]
            kind, c0, first = BLOCKS[b]
            if kind == "q":
                o = outs.tile([P, 2, HD], F32, name="o", bufs=4)
                dst = q_rows[first : first + 2, t].rearrange("s p c -> p s c")
                u = work.tile([P, BLOCK], F32, name="u", bufs=4)
                nc.scalar.copy(out=u[:], in_=acc)
                rotate(n, u[:], o[:].rearrange("p s c -> p (s c)"), [(nc.gpsimd, dst, o[:])])
                return
            if t % 2 == 0:
                pair["k"] = outs.tile([P, 2, HD], F32, name="ko", bufs=3)
                pair["v"] = outs.tile([P, 2, HD], F32, name="vo", bufs=3)
            ko, vo = pair["k"], pair["v"]
            u = t % 2
            lone = b == 5 and t == TILES - 2
            if lone:
                k_store = [(nc.sync, k_rows[first, t], ko[:, 0, :])]
            elif u == 1:
                k_store = [(nc.gpsimd, k_rows[first, t - 1 : t + 1].rearrange("t p c -> p t c"), ko[:])]
            else:
                k_store = []

            def store_v():
                if lone:
                    nc.sync.dma_start(out=v_rows[first, t], in_=vo[:, 0, :])
                elif u == 1:
                    nc.gpsimd.dma_start(out=v_rows[first, t - 1 : t + 1].rearrange("t p c -> p t c"), in_=vo[:])

            ku = work.tile([P, BLOCK], F32, name="u", bufs=4)
            nc.scalar.copy(out=ku[:, 0:HD], in_=acc[:, 0:HD])
            nc.scalar.copy(out=vo[:, u, :], in_=acc[:, HD : 2 * HD])
            rotate(n, ku[:, 0:HD], ko[:, u, :], k_store, store_v)

        sign_table(0)
        sign_table(1)
        accs = []
        for t in range(8):
            acc = psum.tile([P, BLOCK], F32, name="acc")
            accs.append(acc)
        for g in range(PASSES):
            for t in range(8):
                multiply(accs[t][:], 0, t, g)
        load_weights(1)
        load_tables(1)
        for n in range(8):
            sign_table(n + 2)
            drain(n, accs[n][:])

        for n in range(8, len(groups) - 1):
            b, t = groups[n]
            if t == 0 and b < 5:
                load_weights(b + 1)
                load_tables(b + 1)
            sign_table(n + 2)
            acc = psum.tile([P, BLOCK], F32, name="acc")
            for g in range(PASSES):
                multiply(acc[:], b, t, g)
            drain(n, acc[:])

        n = len(groups) - 1
        b, t = groups[n]
        ko, vo = pair["k"], pair["v"]
        acc_k = psum.tile([P, BLOCK], F32, name="acc")
        acc_v = psum.tile([P, BLOCK], F32, name="acc")
        for g in range(PASSES):
            multiply(acc_k[:, 0:HD], b, t, g, 0, HD)
        for g in range(PASSES):
            multiply(acc_v[:, 0:HD], b, t, g, HD, HD)
        rotate(n, acc_k[:, 0:HD], ko[:, 1, :], [(nc.sync, k_rows[1, t], ko[:, 1, :])])
        flush()
        nc.scalar.copy(out=vo[:, 1, :], in_=acc_v[:, 0:HD])
        nc.scalar.dma_start(out=v_rows[1, t], in_=vo[:, 1, :])
